import numpy as np
import ml_dtypes


def mxq(x, axis, fmt="e4m3"):
    dtype, down = {"e4m3": (ml_dtypes.float8_e4m3fn, 7), "e5m2": (ml_dtypes.float8_e5m2, 14)}[fmt]
    v = np.moveaxis(np.asarray(x, np.float32).astype(ml_dtypes.bfloat16).astype(np.float64), axis, -1)
    blocks = v.reshape(v.shape[:-1] + (-1, 32))
    amax = np.abs(blocks).max(-1, keepdims=True)
    byte = np.maximum(np.where(amax > 0, np.frexp(amax)[1] - 1 + 127, 0) - down, 1)
    scale = np.exp2(byte - 127.0)
    codes = (blocks / scale).astype(np.float32).astype(dtype).astype(np.float64)
    return np.moveaxis((codes * scale).reshape(v.shape), -1, axis)


WIDE = False


def mx_kscale(k):
    if not WIDE:
        return np.ones(k)
    levels = np.array([10, -10, 5, -5, 0])
    if k % 512:
        return np.exp2(np.random.permutation(np.resize(levels, k // 32))).repeat(32)
    a = np.empty((k // 512, 16))
    for p in range(k // 512):
        a[p, :8] = np.random.permutation(np.resize(levels, 8))
        for g in range(8):
            far = levels[np.abs(levels - a[p, g]) >= 10]
            a[p, g + 8] = far[np.random.randint(len(far))]
    return np.exp2(a.ravel()).repeat(32)


BF16 = ml_dtypes.bfloat16


def bf(x):
    return np.asarray(x, np.float32).astype(BF16)


def f64(x):
    return np.asarray(x).astype(np.float64)


E2M1 = np.array([0.0, 0.5, 1.0, 1.5, 2.0, 3.0, 4.0, 6.0, -0.0, -0.5, -1.0, -1.5, -2.0, -3.0, -4.0, -6.0])


def pack_weight(w, fmt):
    k, n = w.shape
    w = f64(bf(w)).reshape(k // 32, 32, n)
    amax = np.abs(w).max(1)
    if fmt == "e4m3":
        byte = np.frexp(amax)[1] - 1 + 127 - 7
    else:
        mant, ex = np.frexp(amax / 6.0)
        byte = np.where(mant > 0.5, ex, ex - 1) + 127
    byte = np.clip(np.where(amax > 0, byte, 1), 1, 254)
    scaled = (w * np.exp2(127.0 - byte)[:, None, :]).reshape(k, n).astype(np.float32)
    by_word = np.ascontiguousarray(scaled.reshape(k // 512, 128, 4, n).transpose(0, 1, 3, 2))
    if fmt == "e4m3":
        words = by_word.astype(ml_dtypes.float8_e4m3fn).view(np.uint8)
    else:
        c = by_word.astype(ml_dtypes.float4_e2m1fn).view(np.uint8) & 0xF
        words = c[..., 0::2] | (c[..., 1::2] << 4)
    return np.ascontiguousarray(words), np.ascontiguousarray(byte.astype(np.uint8).reshape(k // 512, 16, n))


def unpack_weight(words, scales, fmt):
    g, p, n, _ = words.shape
    if fmt == "e4m3":
        vals = np.ascontiguousarray(words).view(ml_dtypes.float8_e4m3fn).astype(np.float64)
    else:
        nib = np.empty((g, p, n, 4), np.uint8)
        nib[..., 0::2] = words & 0xF
        nib[..., 1::2] = words >> 4
        vals = E2M1[nib]
    vals = vals * np.repeat(np.exp2(scales.astype(np.float64) - 127.0), 8, axis=1)[..., None]
    return vals.transpose(0, 1, 3, 2).reshape(g * 512, n)


B, N, NIN, CTX, H, NOUT = 8, 512, 512, 3, 512, 2
F = NIN * CTX


def shift_down(y, d):
    return np.pad(y[:, :-d, :], ((0, 0), (d, 0), (0, 0)))


def shift_up(y, d):
    return np.pad(y[:, d:, :], ((0, 0), (0, d), (0, 0)))


def context_linear(xq, wt, shifts):
    y = xq @ wt[:NIN]
    c = 1
    for d in range(1, CTX // 2 + 1):
        for shift in shifts:
            y = y + shift(xq @ wt[c * NIN:(c + 1) * NIN], d)
            c += 1
    return y


def setup_inputs():
    s, u = mx_kscale(NIN), mx_kscale(H)
    x_l = bf(np.random.standard_normal((B, N, NIN)) * s)
    w_l = np.random.standard_normal((H, F)) / np.sqrt(F) / np.tile(s, CTX) * u[:, None]
    words, scales = pack_weight(np.ascontiguousarray(w_l.T), "e4m3")
    b_l = bf(np.random.standard_normal(H) * 0.3 * u)
    W_bil = bf(np.random.standard_normal((NOUT, H, H)) * 0.2 / np.sqrt(H) / u[None, :, None])
    return {"x_l": x_l, "W_l_words": words, "W_l_scales": scales, "b_l": b_l, "W_bil": W_bil}


def reference(x_l, W_l_words, W_l_scales, b_l, W_bil):
    xq = mxq(f64(x_l), 2, "e4m3")
    hl = np.maximum(context_linear(xq, unpack_weight(W_l_words, W_l_scales, "e4m3"), (shift_down, shift_up)) + f64(b_l), 0.0)
    wb = f64(W_bil).transpose(1, 0, 2).reshape(H, NOUT * H)
    t = mxq(hl, 2, "e4m3") @ mxq(wb, 0, "e4m3")
    return t.reshape(B, N, NOUT, H)

@@ -1,0 +1,259 @@
+from contextlib import ExitStack
+
+import concourse.mybir as mybir
+from concourse.masks import make_identity
+
+F32 = mybir.dt.float32
+BF16 = mybir.dt.bfloat16
+I32 = mybir.dt.int32
+U32 = mybir.dt.uint32
+U8 = mybir.dt.uint8
+FP8X4 = mybir.dt.float8_e4m3fn_x4
+RELU = mybir.ActivationFunctionType.Relu
+
+P = 128
+PACK = 4
+BANK = 512
+
+SEQUENCES = 8
+POSITIONS = 512
+FEATURES = 512
+HIDDEN = 512
+MAPS = 2
+TAPS = 3
+TOKENS = SEQUENCES * POSITIONS
+BLOCKS = TOKENS // P
+SEGMENTS_PER_SEQUENCE = POSITIONS // BLOCKS
+SLOTS = BLOCKS + 2
+PAIRS = SLOTS // 2
+WINDOW = 2
+WINDOW_TOKENS = WINDOW * P
+WINDOWS = BLOCKS // WINDOW
+H_CHUNKS = HIDDEN // P
+X_WORDS = FEATURES // 2
+OUT_COLUMNS = MAPS * HIDDEN
+
+TAP_SLOT = (1, 0, 2)
+
+STEPS = 2 * WINDOWS
+LAYER2_LAG = 4
+FIRST_LAYER2_STEP = 5
+W_BIL_STEP = 1
+TRANSPOSE_EVERY = 4
+
+X_RING = 4
+HQ_RING = 4
+
+FLOPS = 2 * TOKENS * (TAPS * FEATURES * HIDDEN + HIDDEN * OUT_COLUMNS)
+
+
+def tile_bilinearpairedlayer_pa_t_kernel(tc, x_l, W_l_words, W_l_scales, b_l, W_bil, out):
+    nc = tc.nc
+    x_blocks = x_l.rearrange("b (s r) f -> (b s) r f", r=BLOCKS)
+    out_blocks = out.rearrange("b (s r) k g -> (b s) r (k g)", r=BLOCKS)
+
+    with ExitStack() as ctx:
+        ctx.enter_context(tc.manual_schedule())
+        keep = ctx.enter_context(tc.tile_pool(name="keep", bufs=1))
+        results = ctx.enter_context(tc.tile_pool(name="results", bufs=4))
+        psum_t = ctx.enter_context(tc.psum_pool(name="psum_t", bufs=2))
+        psum_1 = ctx.enter_context(tc.psum_pool(name="psum_1", bufs=2))
+        psum_2 = ctx.enter_context(tc.psum_pool(name="psum_2", bufs=4))
+
+        x_sb = keep.tile([P, BLOCKS, FEATURES], BF16)
+        xq_words = keep.tile([P, SLOTS * P], U32, align_bytes=64)
+        xq_scales = keep.tile([P, SLOTS * P], U8, align_bytes=64)
+        w_words = keep.tile([P, TAPS, HIDDEN], U32, align_bytes=64)
+        w_scales = keep.tile([P, TAPS, HIDDEN], U8, align_bytes=64)
+        w_raw_words = keep.tile([P, TAPS, HIDDEN], U32, align_bytes=64)
+        w_raw_scales = keep.tile([P, TAPS, HIDDEN], U8, align_bytes=64)
+        wb_raw = keep.tile([P, MAPS, PACK, HIDDEN], BF16)
+        wb_grouped = keep.tile([P, OUT_COLUMNS, PACK], BF16, align_bytes=64)
+        wbq_words = keep.tile([P, OUT_COLUMNS], U32, align_bytes=64)
+        wbq_scales = keep.tile([P, OUT_COLUMNS], U8, align_bytes=64)
+        identity = keep.tile([P, P], F32)
+        to_next_segment = keep.tile([P, P], F32)
+        to_previous_segment = keep.tile([P, P], F32)
+        bias = keep.tile([P, H_CHUNKS], BF16)
+        x_grouped = keep.tile([P, X_RING, 2, P, PACK], BF16, align_bytes=64)
+        h_planes = keep.tile([P, 2, H_CHUNKS, WINDOW_TOKENS], BF16)
+        h_grouped = keep.tile([P, 2, WINDOW_TOKENS, PACK], BF16, align_bytes=64)
+        hq_words = keep.tile([P, HQ_RING, WINDOW_TOKENS], U32, align_bytes=64)
+        hq_scales = keep.tile([P, HQ_RING, WINDOW_TOKENS], U8, align_bytes=64)
+        x_words = x_sb[:].bitcast(F32)
+
+        nc.vector.memset(w_raw_scales[:].bitcast(I32), 0)
+        nc.vector.memset(to_next_segment[:], 0.0)
+        nc.vector.memset(to_previous_segment[:], 0.0)
+        make_identity(nc, identity[:])
+        by_sequence = "p (b s) -> p b s"
+        nc.vector.tensor_copy(
+            out=to_next_segment[:].rearrange(by_sequence, s=SEGMENTS_PER_SEQUENCE)[:, :, 1:],
+            in_=identity[:].rearrange(by_sequence, s=SEGMENTS_PER_SEQUENCE)[:, :, : SEGMENTS_PER_SEQUENCE - 1],
+        )
+        nc.vector.tensor_copy(
+            out=to_previous_segment[:].rearrange(by_sequence, s=SEGMENTS_PER_SEQUENCE)[:, :, : SEGMENTS_PER_SEQUENCE - 1],
+            in_=identity[:].rearrange(by_sequence, s=SEGMENTS_PER_SEQUENCE)[:, :, 1:],
+        )
+
+        def load_blocks(blocks):
+            nc.sync.dma_start(out=x_sb[:, blocks, :], in_=x_blocks[:, blocks, :])
+
+        def load_pair(pair):
+            load_blocks(slice(2 * pair - 1, 2 * pair + 1))
+
+        def load_weight(tap):
+            nc.sync.dma_start(
+                out=w_raw_words[:, tap, :].bitcast(I32),
+                in_=W_l_words[tap].rearrange("p n t -> p (n t)").bitcast(I32),
+            )
+
+        load_blocks(slice(0, BLOCKS, BLOCKS - 1))
+        load_pair(1)
+        for quadrant in range(4):
+            nc.sync.dma_start(
+                out=w_raw_scales[32 * quadrant : 32 * quadrant + 4, :, :].bitcast(I32),
+                in_=W_l_scales[:, 4 * quadrant : 4 * quadrant + 4, :].rearrange("g r n -> r g n").bitcast(I32),
+            )
+        for tap in range(TAPS):
+            load_weight(tap)
+        nc.sync.dma_start(out=bias[:], in_=b_l.rearrange("(p t) -> p t", t=H_CHUNKS))
+        load_pair(2)
+        load_pair(3)
+        for k in range(MAPS):
+            nc.sync.dma_start(out=wb_raw[:, k], in_=W_bil[k].rearrange("(p t) g -> p t g", t=PACK))
+        for pair in range(4, PAIRS - 1):
+            load_pair(pair)
+
+        def slot_source(slot):
+            if slot == 0:
+                return BLOCKS - 1, to_next_segment
+            if slot == SLOTS - 1:
+                return 0, to_previous_segment
+            return slot - 1, identity
+
+        def transpose_pair(pair):
+            bank = psum_t.tile([P, 2, 2, P], F32, name="bank", tag="transposed")
+            for b in range(2):
+                block, permutation = slot_source(2 * pair + b)
+                for u in range(2):
+                    nc.tensor.transpose(out=bank[:, b, u, :], in_=x_words[:, block, u:X_WORDS:2], identity=permutation[:])
+            copy = nc.scalar.copy if pair % 2 else nc.vector.tensor_copy
+            copy(out=x_grouped[:, pair % X_RING].bitcast(F32), in_=bank[:].rearrange("p b u w -> p b w u"))
+
+        def quantise_pair(pair):
+            columns = slice(2 * pair * P, (2 * pair + 2) * P)
+            nc.vector.quantize_mx(
+                out=xq_words[:, columns].bitcast(FP8X4),
+                scales=xq_scales[:, columns],
+                in_=x_grouped[:, pair % X_RING].rearrange("p b w t -> p (b w t)"),
+            )
+
+        def permute_weight(tap):
+            by_unit, by_chunk = "p (m t) -> p t m", "p (t m) -> p t m"
+            nc.vector.tensor_copy(
+                out=w_words[:, tap, :].bitcast(I32).rearrange(by_chunk, t=H_CHUNKS),
+                in_=w_raw_words[:, tap, :].bitcast(I32).rearrange(by_unit, t=H_CHUNKS),
+            )
+            nc.vector.tensor_copy(
+                out=w_scales[:, tap, :].rearrange(by_chunk, t=H_CHUNKS),
+                in_=w_raw_scales[:, tap, :].rearrange(by_unit, t=H_CHUNKS),
+            )
+
+        def layer1_bank(window, half):
+            groups = psum_1.tile([P, 2, WINDOW_TOKENS], F32, name="groups")
+            for i in range(2):
+                chunk = 2 * half + i
+                units = slice(chunk * P, (chunk + 1) * P)
+                for g in range(TAPS):
+                    first = (window * WINDOW + TAP_SLOT[g]) * P
+                    nc.tensor.matmul_mx(
+                        out=groups[:, i, :],
+                        lhsT=w_words[:, g, units].bitcast(FP8X4),
+                        lhsT_scale=w_scales[:, g, units],
+                        rhs=xq_words[:, first : first + WINDOW_TOKENS].bitcast(FP8X4),
+                        rhs_scale=xq_scales[:, first : first + WINDOW_TOKENS],
+                        start=(g == 0),
+                        stop=(g == TAPS - 1),
+                    )
+            for i in range(2):
+                chunk = 2 * half + i
+                nc.scalar.activation(
+                    out=h_planes[:, window % 2, chunk, :],
+                    in_=groups[:, i, :],
+                    func=RELU,
+                    bias=bias[:, chunk : chunk + 1],
+                    scale=1.0,
+                )
+
+        def regroup(grouped, planes):
+            nc.vector.tensor_copy(
+                out=grouped.rearrange("p (c i) t -> p c t i", i=4), in_=planes.rearrange("p t (c i) -> p c t i", i=4)
+            )
+
+        def quantise_hidden(window):
+            nc.vector.quantize_mx(
+                out=hq_words[:, window % HQ_RING, :].bitcast(FP8X4),
+                scales=hq_scales[:, window % HQ_RING, :],
+                in_=h_grouped[:, window % 2].rearrange("p w t -> p (w t)"),
+            )
+
+        def quantise_w_bil():
+            for k in range(MAPS):
+                columns = slice(k * HIDDEN, (k + 1) * HIDDEN)
+                regroup(wb_grouped[:, columns, :], wb_raw[:, k])
+            for k in range(MAPS):
+                columns = slice(k * HIDDEN, (k + 1) * HIDDEN)
+                nc.vector.quantize_mx(
+                    out=wbq_words[:, columns].bitcast(FP8X4),
+                    scales=wbq_scales[:, columns],
+                    in_=wb_grouped[:, columns, :].rearrange("p n t -> p (n t)"),
+                )
+
+        def layer2_block(block):
+            window, place = divmod(block, WINDOW)
+            tokens = slice(place * P, (place + 1) * P)
+            result = results.tile([P, OUT_COLUMNS], F32, name="result")
+            for k, copy in enumerate((nc.scalar.copy, nc.vector.tensor_copy)):
+                columns = slice(k * HIDDEN, (k + 1) * HIDDEN)
+                product = psum_2.tile([P, BANK], F32, name="product")
+                nc.tensor.matmul_mx(
+                    out=product[:],
+                    lhsT=hq_words[:, window % HQ_RING, tokens].bitcast(FP8X4),
+                    lhsT_scale=hq_scales[:, window % HQ_RING, tokens],
+                    rhs=wbq_words[:, columns].bitcast(FP8X4),
+                    rhs_scale=wbq_scales[:, columns],
+                    start=True,
+                    stop=True,
+                )
+                copy(out=result[:, columns], in_=product[:])
+            nc.sync.dma_start(out=out_blocks[:, block, :], in_=result[:])
+
+        transpose_pair(0)
+        transpose_pair(1)
+        quantise_pair(0)
+        quantise_pair(1)
+        for tap in range(TAPS):
+            permute_weight(tap)
+
+        next_block = 0
+        for step in range(STEPS + LAYER2_LAG):
+            window, half = divmod(step, 2)
+            finished = window - 1
+            if half == 0 and 0 <= finished < WINDOWS:
+                regroup(h_grouped[:, finished % 2], h_planes[:, finished % 2])
+            if half == 1 and 0 <= finished < WINDOWS:
+                quantise_hidden(finished)
+            run = [pair for pair in (step // 2 + 2, step // 2 + 3) if step % TRANSPOSE_EVERY == 0 and pair < PAIRS]
+            for pair in run:
+                transpose_pair(pair)
+            if step == W_BIL_STEP:
+                quantise_w_bil()
+            if step < STEPS:
+                layer1_bank(window, half)
+            for turn in range(2):
+                if step >= FIRST_LAYER2_STEP and next_block < BLOCKS and next_block + LAYER2_LAG <= step:
+                    layer2_block(next_block)
+                    next_block += 1
+            for pair in run:
+                quantise_pair(pair)

@@ -37,12 +37,14 @@ TAP_SLOT = (1, 0, 2)
 
 STEPS = 2 * WINDOWS
 LAYER2_LAG = 4
-FIRST_LAYER2_STEP = 5
-W_BIL_STEP = 1
+FIRST_LAYER2_STEP = 10
+FIRST_W_BIL_STEP = 1
+W_BIL_PIECES = 8
+W_BIL_PIECE = OUT_COLUMNS // W_BIL_PIECES
 TRANSPOSE_EVERY = 4
 
 X_RING = 4
-HQ_RING = 4
+HQ_RING = 8
 
 FLOPS = 2 * TOKENS * (TAPS * FEATURES * HIDDEN + HIDDEN * OUT_COLUMNS)
 
@@ -71,6 +73,7 @@ def tile_bilinearpairedlayer_pa_t_kernel(tc, x_l, W_l_words, W_l_scales, b_l, W_
         wb_grouped = keep.tile([P, OUT_COLUMNS, PACK], BF16, align_bytes=64)
         wbq_words = keep.tile([P, OUT_COLUMNS], U32, align_bytes=64)
         wbq_scales = keep.tile([P, OUT_COLUMNS], U8, align_bytes=64)
+        zeros = keep.tile([P, BANK], BF16)
         identity = keep.tile([P, P], F32)
         to_next_segment = keep.tile([P, P], F32)
         to_previous_segment = keep.tile([P, P], F32)
@@ -85,7 +88,9 @@ def tile_bilinearpairedlayer_pa_t_kernel(tc, x_l, W_l_words, W_l_scales, b_l, W_
         nc.vector.memset(w_raw_scales[:].bitcast(I32), 0)
         nc.vector.memset(to_next_segment[:], 0.0)
         nc.vector.memset(to_previous_segment[:], 0.0)
+        nc.gpsimd.memset(zeros[:], 0.0)
         make_identity(nc, identity[:])
+        nc.gpsimd.dma_start(out=bias[:], in_=b_l.rearrange("(p t) -> p t", t=H_CHUNKS))
         by_sequence = "p (b s) -> p b s"
         nc.vector.tensor_copy(
             out=to_next_segment[:].rearrange(by_sequence, s=SEGMENTS_PER_SEQUENCE)[:, :, 1:],
@@ -102,10 +107,10 @@ def tile_bilinearpairedlayer_pa_t_kernel(tc, x_l, W_l_words, W_l_scales, b_l, W_
         def load_pair(pair):
             load_blocks(slice(2 * pair - 1, 2 * pair + 1))
 
-        def load_weight(tap):
+        def load_weight(taps):
             nc.sync.dma_start(
-                out=w_raw_words[:, tap, :].bitcast(I32),
-                in_=W_l_words[tap].rearrange("p n t -> p (n t)").bitcast(I32),
+                out=w_raw_words[:, taps, :].bitcast(I32),
+                in_=W_l_words[taps].rearrange("g p n t -> p g (n t)").bitcast(I32),
             )
 
         load_blocks(slice(0, BLOCKS, BLOCKS - 1))
@@ -115,11 +120,9 @@ def tile_bilinearpairedlayer_pa_t_kernel(tc, x_l, W_l_words, W_l_scales, b_l, W_
                 out=w_raw_scales[32 * quadrant : 32 * quadrant + 4, :, :].bitcast(I32),
                 in_=W_l_scales[:, 4 * quadrant : 4 * quadrant + 4, :].rearrange("g r n -> r g n").bitcast(I32),
             )
-        for tap in range(TAPS):
-            load_weight(tap)
-        nc.sync.dma_start(out=bias[:], in_=b_l.rearrange("(p t) -> p t", t=H_CHUNKS))
-        load_pair(2)
-        load_pair(3)
+        load_weight(slice(0, 1))
+        load_weight(slice(1, TAPS))
+        load_blocks(slice(3, 7))
         for k in range(MAPS):
             nc.sync.dma_start(out=wb_raw[:, k], in_=W_bil[k].rearrange("(p t) g -> p t g", t=PACK))
         for pair in range(4, PAIRS - 1):
@@ -138,8 +141,7 @@ def tile_bilinearpairedlayer_pa_t_kernel(tc, x_l, W_l_words, W_l_scales, b_l, W_
                 block, permutation = slot_source(2 * pair + b)
                 for u in range(2):
                     nc.tensor.transpose(out=bank[:, b, u, :], in_=x_words[:, block, u:X_WORDS:2], identity=permutation[:])
-            copy = nc.scalar.copy if pair % 2 else nc.vector.tensor_copy
-            copy(out=x_grouped[:, pair % X_RING].bitcast(F32), in_=bank[:].rearrange("p b u w -> p b w u"))
+            nc.scalar.copy(out=x_grouped[:, pair % X_RING].bitcast(F32), in_=bank[:].rearrange("p b u w -> p b w u"))
 
         def quantise_pair(pair):
             columns = slice(2 * pair * P, (2 * pair + 2) * P)
@@ -149,16 +151,22 @@ def tile_bilinearpairedlayer_pa_t_kernel(tc, x_l, W_l_words, W_l_scales, b_l, W_
                 in_=x_grouped[:, pair % X_RING].rearrange("p b w t -> p (b w t)"),
             )
 
-        def permute_weight(tap):
+        def permute_weight(tap, half):
             by_unit, by_chunk = "p (m t) -> p t m", "p (t m) -> p t m"
+            chunks = slice(2 * half, 2 * half + 2)
             nc.vector.tensor_copy(
-                out=w_words[:, tap, :].bitcast(I32).rearrange(by_chunk, t=H_CHUNKS),
-                in_=w_raw_words[:, tap, :].bitcast(I32).rearrange(by_unit, t=H_CHUNKS),
+                out=w_words[:, tap, :].bitcast(I32).rearrange(by_chunk, t=H_CHUNKS)[:, chunks],
+                in_=w_raw_words[:, tap, :].bitcast(I32).rearrange(by_unit, t=H_CHUNKS)[:, chunks],
             )
             nc.vector.tensor_copy(
-                out=w_scales[:, tap, :].rearrange(by_chunk, t=H_CHUNKS),
-                in_=w_raw_scales[:, tap, :].rearrange(by_unit, t=H_CHUNKS),
+                out=w_scales[:, tap, :].rearrange(by_chunk, t=H_CHUNKS)[:, chunks],
+                in_=w_raw_scales[:, tap, :].rearrange(by_unit, t=H_CHUNKS)[:, chunks],
             )
+
+        def keep_warm(count):
+            for turn in range(count):
+                scratch = psum_2.tile([P, BANK], F32, name="scratch", tag="product")
+                nc.tensor.matmul(out=scratch[:], lhsT=zeros[:, 0:P], rhs=zeros[:], start=True, stop=True)
 
         def layer1_bank(window, half):
             groups = psum_1.tile([P, 2, WINDOW_TOKENS], F32, name="groups")
@@ -198,17 +206,20 @@ def tile_bilinearpairedlayer_pa_t_kernel(tc, x_l, W_l_words, W_l_scales, b_l, W_
                 in_=h_grouped[:, window % 2].rearrange("p w t -> p (w t)"),
             )
 
-        def quantise_w_bil():
-            for k in range(MAPS):
-                columns = slice(k * HIDDEN, (k + 1) * HIDDEN)
-                regroup(wb_grouped[:, columns, :], wb_raw[:, k])
-            for k in range(MAPS):
-                columns = slice(k * HIDDEN, (k + 1) * HIDDEN)
-                nc.vector.quantize_mx(
-                    out=wbq_words[:, columns].bitcast(FP8X4),
-                    scales=wbq_scales[:, columns],
-                    in_=wb_grouped[:, columns, :].rearrange("p n t -> p (n t)"),
-                )
+        def regroup_w_bil(piece):
+            k, place = divmod(piece * W_BIL_PIECE, HIDDEN)
+            regroup(
+                wb_grouped[:, piece * W_BIL_PIECE : (piece + 1) * W_BIL_PIECE, :],
+                wb_raw[:, k, :, place : place + W_BIL_PIECE],
+            )
+
+        def quantise_w_bil(piece):
+            columns = slice(piece * W_BIL_PIECE, (piece + 1) * W_BIL_PIECE)
+            nc.vector.quantize_mx(
+                out=wbq_words[:, columns].bitcast(FP8X4),
+                scales=wbq_scales[:, columns],
+                in_=wb_grouped[:, columns, :].rearrange("p n t -> p (n t)"),
+            )
 
         def layer2_block(block):
             window, place = divmod(block, WINDOW)
@@ -216,7 +227,7 @@ def tile_bilinearpairedlayer_pa_t_kernel(tc, x_l, W_l_words, W_l_scales, b_l, W_
             result = results.tile([P, OUT_COLUMNS], F32, name="result")
             for k, copy in enumerate((nc.scalar.copy, nc.vector.tensor_copy)):
                 columns = slice(k * HIDDEN, (k + 1) * HIDDEN)
-                product = psum_2.tile([P, BANK], F32, name="product")
+                product = psum_2.tile([P, BANK], F32, name="product", tag="product")
                 nc.tensor.matmul_mx(
                     out=product[:],
                     lhsT=hq_words[:, window % HQ_RING, tokens].bitcast(FP8X4),
@@ -229,12 +240,17 @@ def tile_bilinearpairedlayer_pa_t_kernel(tc, x_l, W_l_words, W_l_scales, b_l, W_
                 copy(out=result[:, columns], in_=product[:])
             nc.sync.dma_start(out=out_blocks[:, block, :], in_=result[:])
 
+        keep_warm(3)
         transpose_pair(0)
         transpose_pair(1)
+        keep_warm(6)
+        permute_weight(0, 0)
         quantise_pair(0)
+        permute_weight(1, 0)
         quantise_pair(1)
+        permute_weight(2, 0)
         for tap in range(TAPS):
-            permute_weight(tap)
+            permute_weight(tap, 1)
 
         next_block = 0
         for step in range(STEPS + LAYER2_LAG):
@@ -245,12 +261,17 @@ def tile_bilinearpairedlayer_pa_t_kernel(tc, x_l, W_l_words, W_l_scales, b_l, W_
             if half == 1 and 0 <= finished < WINDOWS:
                 quantise_hidden(finished)
             run = [pair for pair in (step // 2 + 2, step // 2 + 3) if step % TRANSPOSE_EVERY == 0 and pair < PAIRS]
+            if step == 0:
+                layer1_bank(window, half)
             for pair in run:
                 transpose_pair(pair)
-            if step == W_BIL_STEP:
-                quantise_w_bil()
-            if step < STEPS:
+            if 0 < step < STEPS:
                 layer1_bank(window, half)
+            piece = step - FIRST_W_BIL_STEP
+            if 0 <= piece - 1 < W_BIL_PIECES:
+                quantise_w_bil(piece - 1)
+            if 0 <= piece < W_BIL_PIECES:
+                regroup_w_bil(piece)
             for turn in range(2):
                 if step >= FIRST_LAYER2_STEP and next_block < BLOCKS and next_block + LAYER2_LAG <= step:
                     layer2_block(next_block)

@@ -28,22 +28,24 @@ SLOTS = BLOCKS + 2
 PAIRS = SLOTS // 2
 WINDOW = 2
 WINDOW_TOKENS = WINDOW * P
-WINDOWS = BLOCKS // WINDOW
 H_CHUNKS = HIDDEN // P
 X_WORDS = FEATURES // 2
 OUT_COLUMNS = MAPS * HIDDEN
 
 TAP_SLOT = (1, 0, 2)
 
-STEPS = 2 * WINDOWS
-LAYER2_LAG = 4
-FIRST_LAYER2_STEP = 10
+WINDOW_STEPS = [(2 * w, 2, half) for w in range(BLOCKS // 2 - 1) for half in range(2)]
+STEPS = [(first, blocks, 2 * half, 2) for first, blocks, half in WINDOW_STEPS] + [
+    (block, 1, 0, H_CHUNKS) for block in range(BLOCKS - 2, BLOCKS)
+]
+LAYER2_LAG = 3
+FIRST_LAYER2_STEP = 6
 FIRST_W_BIL_STEP = 1
-W_BIL_PIECES = 8
+W_BIL_PIECES = 4
 W_BIL_PIECE = OUT_COLUMNS // W_BIL_PIECES
-TRANSPOSE_EVERY = 4
-
-X_RING = 4
+RUNS = ((0, (2, 3,)), (3, (4, 5,)), (7, (6, 7,)), (11, (8, 9,)), (15, (10, 11,)), (19, (12, 13,)), (23, (14, 15,)), (27, (16,)))
+SPLIT_PAIRS = range(6, PAIRS - 1)
+X_RING = 6
 HQ_RING = 8
 
 FLOPS = 2 * TOKENS * (TAPS * FEATURES * HIDDEN + HIDDEN * OUT_COLUMNS)
@@ -78,6 +80,7 @@ def tile_bilinearpairedlayer_pa_t_kernel(tc, x_l, W_l_words, W_l_scales, b_l, W_
         to_next_segment = keep.tile([P, P], F32)
         to_previous_segment = keep.tile([P, P], F32)
         bias = keep.tile([P, H_CHUNKS], BF16)
+        x_split = keep.tile([P, BLOCKS, 2, P], F32)
         x_grouped = keep.tile([P, X_RING, 2, P, PACK], BF16, align_bytes=64)
         h_planes = keep.tile([P, 2, H_CHUNKS, WINDOW_TOKENS], BF16)
         h_grouped = keep.tile([P, 2, WINDOW_TOKENS, PACK], BF16, align_bytes=64)
@@ -135,13 +138,22 @@ def tile_bilinearpairedlayer_pa_t_kernel(tc, x_l, W_l_words, W_l_scales, b_l, W_
                 return 0, to_previous_segment
             return slot - 1, identity
 
+        def split_pair(pair):
+            blocks = slice(2 * pair - 1, 2 * pair + 1)
+            nc.vector.tensor_copy(
+                out=x_split[:, blocks], in_=x_words[:, blocks].rearrange("p b (w u) -> p b u w", u=2)
+            )
+
         def transpose_pair(pair):
-            bank = psum_t.tile([P, 2, 2, P], F32, name="bank", tag="transposed")
+            bank = banks[pair] = psum_t.tile([P, 2, 2, P], F32, name="bank", tag="transposed")
             for b in range(2):
                 block, permutation = slot_source(2 * pair + b)
                 for u in range(2):
-                    nc.tensor.transpose(out=bank[:, b, u, :], in_=x_words[:, block, u:X_WORDS:2], identity=permutation[:])
-            nc.scalar.copy(out=x_grouped[:, pair % X_RING].bitcast(F32), in_=bank[:].rearrange("p b u w -> p b w u"))
+                    words = x_split[:, block, u, :] if pair in SPLIT_PAIRS else x_words[:, block, u:X_WORDS:2]
+                    nc.tensor.transpose(out=bank[:, b, u, :], in_=words, identity=permutation[:])
+
+        def empty_pair(pair, copy=nc.scalar.copy):
+            copy(out=x_grouped[:, pair % X_RING].bitcast(F32), in_=banks[pair][:].rearrange("p b u w -> p b w u"))
 
         def quantise_pair(pair):
             columns = slice(2 * pair * P, (2 * pair + 2) * P)
@@ -168,42 +180,45 @@ def tile_bilinearpairedlayer_pa_t_kernel(tc, x_l, W_l_words, W_l_scales, b_l, W_
                 scratch = psum_2.tile([P, BANK], F32, name="scratch", tag="product")
                 nc.tensor.matmul(out=scratch[:], lhsT=zeros[:, 0:P], rhs=zeros[:], start=True, stop=True)
 
-        def layer1_bank(window, half):
-            groups = psum_1.tile([P, 2, WINDOW_TOKENS], F32, name="groups")
-            for i in range(2):
-                chunk = 2 * half + i
-                units = slice(chunk * P, (chunk + 1) * P)
+        def layer1_bank(first, blocks, chunk0, chunks):
+            tokens = blocks * P
+            groups = psum_1.tile([P, chunks, tokens], F32, name="groups")
+            for i in range(chunks):
+                units = slice((chunk0 + i) * P, (chunk0 + i + 1) * P)
                 for g in range(TAPS):
-                    first = (window * WINDOW + TAP_SLOT[g]) * P
+                    column = (first + TAP_SLOT[g]) * P
                     nc.tensor.matmul_mx(
                         out=groups[:, i, :],
                         lhsT=w_words[:, g, units].bitcast(FP8X4),
                         lhsT_scale=w_scales[:, g, units],
-                        rhs=xq_words[:, first : first + WINDOW_TOKENS].bitcast(FP8X4),
-                        rhs_scale=xq_scales[:, first : first + WINDOW_TOKENS],
+                        rhs=xq_words[:, column : column + tokens].bitcast(FP8X4),
+                        rhs_scale=xq_scales[:, column : column + tokens],
                         start=(g == 0),
                         stop=(g == TAPS - 1),
                     )
-            for i in range(2):
-                chunk = 2 * half + i
+            for i in range(chunks):
+                chunk = chunk0 + i
                 nc.scalar.activation(
-                    out=h_planes[:, window % 2, chunk, :],
+                    out=h_planes[:, first // 2 % 2, chunk, first % 2 * P : first % 2 * P + tokens],
                     in_=groups[:, i, :],
                     func=RELU,
                     bias=bias[:, chunk : chunk + 1],
                     scale=1.0,
                 )
 
-        def regroup(grouped, planes):
-            nc.vector.tensor_copy(
-                out=grouped.rearrange("p (c i) t -> p c t i", i=4), in_=planes.rearrange("p t (c i) -> p c t i", i=4)
-            )
+        def regroup(grouped, planes, copy=nc.vector.tensor_copy):
+            copy(out=grouped.rearrange("p (c i) t -> p c t i", i=4), in_=planes.rearrange("p t (c i) -> p c t i", i=4))
 
-        def quantise_hidden(window):
+        def regroup_hidden(first, blocks):
+            columns = slice(first % 2 * P, (first % 2 + blocks) * P)
+            regroup(h_grouped[:, first // 2 % 2, columns], h_planes[:, first // 2 % 2, :, columns])
+
+        def quantise_hidden(first, blocks):
+            columns = slice(first % 2 * P, (first % 2 + blocks) * P)
             nc.vector.quantize_mx(
-                out=hq_words[:, window % HQ_RING, :].bitcast(FP8X4),
-                scales=hq_scales[:, window % HQ_RING, :],
-                in_=h_grouped[:, window % 2].rearrange("p w t -> p (w t)"),
+                out=hq_words[:, first // 2 % HQ_RING, columns].bitcast(FP8X4),
+                scales=hq_scales[:, first // 2 % HQ_RING, columns],
+                in_=h_grouped[:, first // 2 % 2, columns].rearrange("p w t -> p (w t)"),
             )
 
         def regroup_w_bil(piece):
@@ -211,6 +226,7 @@ def tile_bilinearpairedlayer_pa_t_kernel(tc, x_l, W_l_words, W_l_scales, b_l, W_
             regroup(
                 wb_grouped[:, piece * W_BIL_PIECE : (piece + 1) * W_BIL_PIECE, :],
                 wb_raw[:, k, :, place : place + W_BIL_PIECE],
+                nc.scalar.copy if piece % 2 else nc.vector.tensor_copy,
             )
 
         def quantise_w_bil(piece):
@@ -240,41 +256,56 @@ def tile_bilinearpairedlayer_pa_t_kernel(tc, x_l, W_l_words, W_l_scales, b_l, W_
                 copy(out=result[:, columns], in_=product[:])
             nc.sync.dma_start(out=out_blocks[:, block, :], in_=result[:])
 
+        banks = {}
         keep_warm(3)
         transpose_pair(0)
+        empty_pair(0)
         transpose_pair(1)
+        empty_pair(1)
         keep_warm(6)
         permute_weight(0, 0)
         quantise_pair(0)
-        permute_weight(1, 0)
         quantise_pair(1)
+        permute_weight(1, 0)
         permute_weight(2, 0)
         for tap in range(TAPS):
             permute_weight(tap, 1)
 
         next_block = 0
-        for step in range(STEPS + LAYER2_LAG):
-            window, half = divmod(step, 2)
-            finished = window - 1
-            if half == 0 and 0 <= finished < WINDOWS:
-                regroup(h_grouped[:, finished % 2], h_planes[:, finished % 2])
-            if half == 1 and 0 <= finished < WINDOWS:
-                quantise_hidden(finished)
-            run = [pair for pair in (step // 2 + 2, step // 2 + 3) if step % TRANSPOSE_EVERY == 0 and pair < PAIRS]
+        last = len(STEPS) - 1
+        for step in range(len(STEPS) + LAYER2_LAG):
+            complete = None
+            if 1 <= step <= last + 1:
+                first, blocks, chunk0, chunks = STEPS[step - 1]
+                if chunk0 + chunks == H_CHUNKS:
+                    complete = (first, blocks)
+            if complete:
+                regroup_hidden(*complete)
+            for start, pairs in RUNS:
+                if 1 <= step - start <= len(pairs):
+                    quantise_pair(pairs[step - start - 1])
+                for i, pair in enumerate(pairs):
+                    if step == start - 2 - (len(pairs) - 1 - i) * 2 and pair in SPLIT_PAIRS:
+                        split_pair(pair)
+            if complete:
+                quantise_hidden(*complete)
             if step == 0:
-                layer1_bank(window, half)
-            for pair in run:
-                transpose_pair(pair)
-            if 0 < step < STEPS:
-                layer1_bank(window, half)
+                layer1_bank(*STEPS[step])
+            for start, pairs in RUNS:
+                if step == start:
+                    for pair in pairs:
+                        transpose_pair(pair)
+                        pass
+                if 0 <= step - start < len(pairs):
+                    empty_pair(pairs[step - start])
+            if 0 < step <= last:
+                layer1_bank(*STEPS[step])
+            for turn in range(2):
+                if step >= FIRST_LAYER2_STEP and next_block < BLOCKS and next_block + LAYER2_LAG <= step:
+                    layer2_block(next_block)
+                    next_block += 1
             piece = step - FIRST_W_BIL_STEP
             if 0 <= piece - 1 < W_BIL_PIECES:
                 quantise_w_bil(piece - 1)
             if 0 <= piece < W_BIL_PIECES:
                 regroup_w_bil(piece)
-            for turn in range(2):
-                if step >= FIRST_LAYER2_STEP and next_block < BLOCKS and next_block + LAYER2_LAG <= step:
-                    layer2_block(next_block)
-                    next_block += 1
-            for pair in run:
-                quantise_pair(pair)

@@ -38,13 +38,13 @@ WINDOW_STEPS = [(2 * w, 2, half) for w in range(BLOCKS // 2 - 1) for half in ran
 STEPS = [(first, blocks, 2 * half, 2) for first, blocks, half in WINDOW_STEPS] + [
     (block, 1, 0, H_CHUNKS) for block in range(BLOCKS - 2, BLOCKS)
 ]
-LAYER2_LAG = 3
-FIRST_LAYER2_STEP = 6
+LAYER2_LAG = 4
+FIRST_LAYER2_STEP = 5
 FIRST_W_BIL_STEP = 1
 W_BIL_PIECES = 4
 W_BIL_PIECE = OUT_COLUMNS // W_BIL_PIECES
-RUNS = ((0, (2, 3,)), (3, (4, 5,)), (7, (6, 7,)), (11, (8, 9,)), (15, (10, 11,)), (19, (12, 13,)), (23, (14, 15,)), (27, (16,)))
-SPLIT_PAIRS = range(6, PAIRS - 1)
+RUNS = ((0, (2, 3,)), (4, (4, 5, 6, 7,)), (12, (8, 9, 10, 11,)), (20, (12, 13, 14, 15,)), (28, (16,)))
+SPLIT_PAIRS = range(8, PAIRS - 1)
 X_RING = 6
 HQ_RING = 8
 
@@ -59,10 +59,9 @@ def tile_bilinearpairedlayer_pa_t_kernel(tc, x_l, W_l_words, W_l_scales, b_l, W_
     with ExitStack() as ctx:
         ctx.enter_context(tc.manual_schedule())
         keep = ctx.enter_context(tc.tile_pool(name="keep", bufs=1))
-        results = ctx.enter_context(tc.tile_pool(name="results", bufs=4))
-        psum_t = ctx.enter_context(tc.psum_pool(name="psum_t", bufs=2))
+        results = ctx.enter_context(tc.tile_pool(name="results", bufs=8))
         psum_1 = ctx.enter_context(tc.psum_pool(name="psum_1", bufs=2))
-        psum_2 = ctx.enter_context(tc.psum_pool(name="psum_2", bufs=4))
+        psum_2 = ctx.enter_context(tc.psum_pool(name="psum_2", bufs=6))
 
         x_sb = keep.tile([P, BLOCKS, FEATURES], BF16)
         xq_words = keep.tile([P, SLOTS * P], U32, align_bytes=64)
@@ -124,7 +123,8 @@ def tile_bilinearpairedlayer_pa_t_kernel(tc, x_l, W_l_words, W_l_scales, b_l, W_
                 in_=W_l_scales[:, 4 * quadrant : 4 * quadrant + 4, :].rearrange("g r n -> r g n").bitcast(I32),
             )
         load_weight(slice(0, 1))
-        load_weight(slice(1, TAPS))
+        load_weight(slice(1, 2))
+        load_weight(slice(2, 3))
         load_blocks(slice(3, 7))
         for k in range(MAPS):
             nc.sync.dma_start(out=wb_raw[:, k], in_=W_bil[k].rearrange("(p t) g -> p t g", t=PACK))
@@ -145,7 +145,7 @@ def tile_bilinearpairedlayer_pa_t_kernel(tc, x_l, W_l_words, W_l_scales, b_l, W_
             )
 
         def transpose_pair(pair):
-            bank = banks[pair] = psum_t.tile([P, 2, 2, P], F32, name="bank", tag="transposed")
+            bank = banks[pair] = psum_2.tile([P, 2, 2, P], F32, name="bank", tag="product")
             for b in range(2):
                 block, permutation = slot_source(2 * pair + b)
                 for u in range(2):
@@ -262,9 +262,9 @@ def tile_bilinearpairedlayer_pa_t_kernel(tc, x_l, W_l_words, W_l_scales, b_l, W_
         empty_pair(0)
         transpose_pair(1)
         empty_pair(1)
-        keep_warm(6)
-        permute_weight(0, 0)
+        keep_warm(4)
         quantise_pair(0)
+        permute_weight(0, 0)
         quantise_pair(1)
         permute_weight(1, 0)
         permute_weight(2, 0)
@@ -285,27 +285,26 @@ def tile_bilinearpairedlayer_pa_t_kernel(tc, x_l, W_l_words, W_l_scales, b_l, W_
                 if 1 <= step - start <= len(pairs):
                     quantise_pair(pairs[step - start - 1])
                 for i, pair in enumerate(pairs):
-                    if step == start - 2 - (len(pairs) - 1 - i) * 2 and pair in SPLIT_PAIRS:
+                    if step == start - 1 - (len(pairs) - 1 - i) * 1 and pair in SPLIT_PAIRS:
                         split_pair(pair)
             if complete:
                 quantise_hidden(*complete)
             if step == 0:
                 layer1_bank(*STEPS[step])
+            piece = step - FIRST_W_BIL_STEP
+            if 0 <= piece < W_BIL_PIECES:
+                regroup_w_bil(piece)
             for start, pairs in RUNS:
                 if step == start:
                     for pair in pairs:
                         transpose_pair(pair)
-                        pass
-                if 0 <= step - start < len(pairs):
-                    empty_pair(pairs[step - start])
+                        empty_pair(pair)
+
             if 0 < step <= last:
                 layer1_bank(*STEPS[step])
-            for turn in range(2):
-                if step >= FIRST_LAYER2_STEP and next_block < BLOCKS and next_block + LAYER2_LAG <= step:
-                    layer2_block(next_block)
-                    next_block += 1
-            piece = step - FIRST_W_BIL_STEP
             if 0 <= piece - 1 < W_BIL_PIECES:
                 quantise_w_bil(piece - 1)
-            if 0 <= piece < W_BIL_PIECES:
-                regroup_w_bil(piece)
+            for turn in range(2):
+                if step >= FIRST_LAYER2_STEP and next_block < BLOCKS and next_block + (4 if step < 26 else 3) <= step:
+                    layer2_block(next_block)
+                    next_block += 1

@@ -34,17 +34,17 @@ OUT_COLUMNS = MAPS * HIDDEN
 
 TAP_SLOT = (1, 0, 2)
 
-WINDOW_STEPS = [(2 * w, 2, half) for w in range(BLOCKS // 2 - 1) for half in range(2)]
+WINDOW_STEPS = [(2 * w, 2, half) for w in range(BLOCKS // 2 - 2) for half in range(2)]
 STEPS = [(first, blocks, 2 * half, 2) for first, blocks, half in WINDOW_STEPS] + [
-    (block, 1, 0, H_CHUNKS) for block in range(BLOCKS - 2, BLOCKS)
+    (block, 1, 0, H_CHUNKS) for block in range(BLOCKS - 4, BLOCKS)
 ]
 LAYER2_LAG = 4
 FIRST_LAYER2_STEP = 5
 FIRST_W_BIL_STEP = 1
 W_BIL_PIECES = 4
 W_BIL_PIECE = OUT_COLUMNS // W_BIL_PIECES
-RUNS = ((0, (2, 3,)), (4, (4, 5, 6, 7,)), (12, (8, 9, 10, 11,)), (20, (12, 13, 14, 15,)), (28, (16,)))
-SPLIT_PAIRS = range(8, PAIRS - 1)
+RUNS = ((0, (2, 3,)), (4, (4, 5, 6,)), (10, (7, 8, 9,)), (16, (10, 11, 12,)), (22, (13, 14, 15,)), (28, (16,)))
+SPLIT_PAIRS = range(6, PAIRS - 1)
 X_RING = 6
 HQ_RING = 8
 
@@ -254,7 +254,10 @@ def tile_bilinearpairedlayer_pa_t_kernel(tc, x_l, W_l_words, W_l_scales, b_l, W_
                     stop=True,
                 )
                 copy(out=result[:, columns], in_=product[:])
-            nc.sync.dma_start(out=out_blocks[:, block, :], in_=result[:])
+            pieces = 1 if block < BLOCKS - 2 else MAPS
+            for piece in range(pieces):
+                columns = slice(piece * OUT_COLUMNS // pieces, (piece + 1) * OUT_COLUMNS // pieces)
+                nc.sync.dma_start(out=out_blocks[:, block, columns], in_=result[:, columns])
 
         banks = {}
         keep_warm(3)
@@ -305,6 +308,6 @@ def tile_bilinearpairedlayer_pa_t_kernel(tc, x_l, W_l_words, W_l_scales, b_l, W_
             if 0 <= piece - 1 < W_BIL_PIECES:
                 quantise_w_bil(piece - 1)
             for turn in range(2):
-                if step >= FIRST_LAYER2_STEP and next_block < BLOCKS and next_block + (4 if step < 26 else 3) <= step:
+                if step >= FIRST_LAYER2_STEP and next_block < BLOCKS and (next_block + 4 <= step if step < 26 else (next_block if next_block >= BLOCKS - 4 else next_block // 2 * 2 + 1) + 2 <= step):
                     layer2_block(next_block)
                     next_block += 1

@@ -43,7 +43,7 @@ FIRST_LAYER2_STEP = 5
 FIRST_W_BIL_STEP = 1
 W_BIL_PIECES = 4
 W_BIL_PIECE = OUT_COLUMNS // W_BIL_PIECES
-RUNS = ((0, (2, 3,)), (4, (4, 5, 6,)), (10, (7, 8, 9,)), (16, (10, 11, 12,)), (22, (13, 14, 15,)), (28, (16,)))
+RUNS = ((0, (2, 3,)), (4, (4, 5,)), (8, (6, 7,)), (12, (8, 9,)), (16, (10, 11,)), (20, (12, 13,)), (24, (14, 15,)), (28, (16,)))
 SPLIT_PAIRS = range(6, PAIRS - 1)
 X_RING = 6
 HQ_RING = 8
@@ -60,8 +60,9 @@ def tile_bilinearpairedlayer_pa_t_kernel(tc, x_l, W_l_words, W_l_scales, b_l, W_
         ctx.enter_context(tc.manual_schedule())
         keep = ctx.enter_context(tc.tile_pool(name="keep", bufs=1))
         results = ctx.enter_context(tc.tile_pool(name="results", bufs=8))
+        psum_t = ctx.enter_context(tc.psum_pool(name="psum_t", bufs=2))
         psum_1 = ctx.enter_context(tc.psum_pool(name="psum_1", bufs=2))
-        psum_2 = ctx.enter_context(tc.psum_pool(name="psum_2", bufs=6))
+        psum_2 = ctx.enter_context(tc.psum_pool(name="psum_2", bufs=4))
 
         x_sb = keep.tile([P, BLOCKS, FEATURES], BF16)
         xq_words = keep.tile([P, SLOTS * P], U32, align_bytes=64)
@@ -145,7 +146,7 @@ def tile_bilinearpairedlayer_pa_t_kernel(tc, x_l, W_l_words, W_l_scales, b_l, W_
             )
 
         def transpose_pair(pair):
-            bank = banks[pair] = psum_2.tile([P, 2, 2, P], F32, name="bank", tag="product")
+            bank = banks[pair] = psum_t.tile([P, 2, 2, P], F32, name="bank", tag="transposed")
             for b in range(2):
                 block, permutation = slot_source(2 * pair + b)
                 for u in range(2):
@@ -288,7 +289,7 @@ def tile_bilinearpairedlayer_pa_t_kernel(tc, x_l, W_l_words, W_l_scales, b_l, W_
                 if 1 <= step - start <= len(pairs):
                     quantise_pair(pairs[step - start - 1])
                 for i, pair in enumerate(pairs):
-                    if step == start - 1 - (len(pairs) - 1 - i) * 1 and pair in SPLIT_PAIRS:
+                    if step == start - 2 - (len(pairs) - 1 - i) * 2 and pair in SPLIT_PAIRS:
                         split_pair(pair)
             if complete:
                 quantise_hidden(*complete)

@@ -26,27 +26,31 @@ BLOCKS = TOKENS // P
 SEGMENTS_PER_SEQUENCE = POSITIONS // BLOCKS
 SLOTS = BLOCKS + 2
 PAIRS = SLOTS // 2
-WINDOW = 2
-WINDOW_TOKENS = WINDOW * P
+GROUP = 4
+GROUP_TOKENS = GROUP * P
 H_CHUNKS = HIDDEN // P
 X_WORDS = FEATURES // 2
 OUT_COLUMNS = MAPS * HIDDEN
 
 TAP_SLOT = (1, 0, 2)
 
-WINDOW_STEPS = [(2 * w, 2, half) for w in range(BLOCKS // 2 - 2) for half in range(2)]
-STEPS = [(first, blocks, 2 * half, 2) for first, blocks, half in WINDOW_STEPS] + [
-    (block, 1, 0, H_CHUNKS) for block in range(BLOCKS - 4, BLOCKS)
+WINDOWS = ((0, 2), (2, 2), (4, 2), (6, 2), (8, 2), (10, 2), (12, 2), (14, 2), (16, 2), (18, 2), (20, 2), (22, 2), (24, 2), (26, 2), (28, 1), (29, 1), (30, 1), (31, 1))
+STEPS = [(first, blocks, chunk, 4 // blocks) for first, blocks in WINDOWS for chunk in range(0, H_CHUNKS, 4 // blocks)]
+FINISHED = [(i, first, blocks) for i, (first, blocks, chunk, chunks) in enumerate(STEPS) if chunk + chunks == H_CHUNKS]
+HALVES = [
+    (first + part, min(blocks, 2), i + 1 + part // 2)
+    for i, first, blocks in FINISHED
+    for part in range(0, blocks, 2)
 ]
-LAYER2_LAG = 4
-FIRST_LAYER2_STEP = 5
+READY = {first + k: ready for first, blocks, ready in HALVES for k in range(blocks)}
+FIRST_LAYER2_STEP = 6
 FIRST_W_BIL_STEP = 1
 W_BIL_PIECES = 4
 W_BIL_PIECE = OUT_COLUMNS // W_BIL_PIECES
-RUNS = ((0, (2, 3,)), (4, (4, 5,)), (8, (6, 7,)), (12, (8, 9,)), (16, (10, 11,)), (20, (12, 13,)), (24, (14, 15,)), (28, (16,)))
-SPLIT_PAIRS = range(6, PAIRS - 1)
+RUNS = ((0, (2, 3,)), (2, (4, 5,)), (6, (6, 7,)), (10, (8, 9,)), (14, (10, 11,)), (18, (12, 13,)), (22, (14, 15,)), (26, (16,)))
+SPLIT_PAIRS = range(8, PAIRS)
 X_RING = 6
-HQ_RING = 8
+HQ_RING = 4
 
 FLOPS = 2 * TOKENS * (TAPS * FEATURES * HIDDEN + HIDDEN * OUT_COLUMNS)
 
@@ -82,10 +86,10 @@ def tile_bilinearpairedlayer_pa_t_kernel(tc, x_l, W_l_words, W_l_scales, b_l, W_
         bias = keep.tile([P, H_CHUNKS], BF16)
         x_split = keep.tile([P, BLOCKS, 2, P], F32)
         x_grouped = keep.tile([P, X_RING, 2, P, PACK], BF16, align_bytes=64)
-        h_planes = keep.tile([P, 2, H_CHUNKS, WINDOW_TOKENS], BF16)
-        h_grouped = keep.tile([P, 2, WINDOW_TOKENS, PACK], BF16, align_bytes=64)
-        hq_words = keep.tile([P, HQ_RING, WINDOW_TOKENS], U32, align_bytes=64)
-        hq_scales = keep.tile([P, HQ_RING, WINDOW_TOKENS], U8, align_bytes=64)
+        h_planes = keep.tile([P, 2, H_CHUNKS, GROUP_TOKENS], BF16)
+        h_grouped = keep.tile([P, 2, GROUP_TOKENS, PACK], BF16, align_bytes=64)
+        hq_words = keep.tile([P, HQ_RING, GROUP_TOKENS], U32, align_bytes=64)
+        hq_scales = keep.tile([P, HQ_RING, GROUP_TOKENS], U8, align_bytes=64)
         x_words = x_sb[:].bitcast(F32)
 
         nc.vector.memset(w_raw_scales[:].bitcast(I32), 0)
@@ -127,9 +131,10 @@ def tile_bilinearpairedlayer_pa_t_kernel(tc, x_l, W_l_words, W_l_scales, b_l, W_
         load_weight(slice(1, 2))
         load_weight(slice(2, 3))
         load_blocks(slice(3, 7))
+        load_blocks(slice(7, 11))
         for k in range(MAPS):
             nc.sync.dma_start(out=wb_raw[:, k], in_=W_bil[k].rearrange("(p t) g -> p t g", t=PACK))
-        for pair in range(4, PAIRS - 1):
+        for pair in range(6, PAIRS - 1):
             load_pair(pair)
 
         def slot_source(slot):
@@ -140,7 +145,7 @@ def tile_bilinearpairedlayer_pa_t_kernel(tc, x_l, W_l_words, W_l_scales, b_l, W_
             return slot - 1, identity
 
         def split_pair(pair):
-            blocks = slice(2 * pair - 1, 2 * pair + 1)
+            blocks = slice(2 * pair - 1, 2 * pair + 1) if pair < PAIRS - 1 else slice(0, BLOCKS, BLOCKS - 1)
             nc.vector.tensor_copy(
                 out=x_split[:, blocks], in_=x_words[:, blocks].rearrange("p b (w u) -> p b u w", u=2)
             )
@@ -200,7 +205,7 @@ def tile_bilinearpairedlayer_pa_t_kernel(tc, x_l, W_l_words, W_l_scales, b_l, W_
             for i in range(chunks):
                 chunk = chunk0 + i
                 nc.scalar.activation(
-                    out=h_planes[:, first // 2 % 2, chunk, first % 2 * P : first % 2 * P + tokens],
+                    out=h_planes[:, first // GROUP % 2, chunk, first % GROUP * P : first % GROUP * P + tokens],
                     in_=groups[:, i, :],
                     func=RELU,
                     bias=bias[:, chunk : chunk + 1],
@@ -211,15 +216,15 @@ def tile_bilinearpairedlayer_pa_t_kernel(tc, x_l, W_l_words, W_l_scales, b_l, W_
             copy(out=grouped.rearrange("p (c i) t -> p c t i", i=4), in_=planes.rearrange("p t (c i) -> p c t i", i=4))
 
         def regroup_hidden(first, blocks):
-            columns = slice(first % 2 * P, (first % 2 + blocks) * P)
-            regroup(h_grouped[:, first // 2 % 2, columns], h_planes[:, first // 2 % 2, :, columns])
+            columns = slice(first % GROUP * P, (first % GROUP + blocks) * P)
+            regroup(h_grouped[:, first // GROUP % 2, columns], h_planes[:, first // GROUP % 2, :, columns])
 
         def quantise_hidden(first, blocks):
-            columns = slice(first % 2 * P, (first % 2 + blocks) * P)
+            columns = slice(first % GROUP * P, (first % GROUP + blocks) * P)
             nc.vector.quantize_mx(
-                out=hq_words[:, first // 2 % HQ_RING, columns].bitcast(FP8X4),
-                scales=hq_scales[:, first // 2 % HQ_RING, columns],
-                in_=h_grouped[:, first // 2 % 2, columns].rearrange("p w t -> p (w t)"),
+                out=hq_words[:, first // GROUP % HQ_RING, columns].bitcast(FP8X4),
+                scales=hq_scales[:, first // GROUP % HQ_RING, columns],
+                in_=h_grouped[:, first // GROUP % 2, columns].rearrange("p w t -> p (w t)"),
             )
 
         def regroup_w_bil(piece):
@@ -227,7 +232,7 @@ def tile_bilinearpairedlayer_pa_t_kernel(tc, x_l, W_l_words, W_l_scales, b_l, W_
             regroup(
                 wb_grouped[:, piece * W_BIL_PIECE : (piece + 1) * W_BIL_PIECE, :],
                 wb_raw[:, k, :, place : place + W_BIL_PIECE],
-                nc.scalar.copy if piece % 2 else nc.vector.tensor_copy,
+                nc.vector.tensor_copy,
             )
 
         def quantise_w_bil(piece):
@@ -239,7 +244,7 @@ def tile_bilinearpairedlayer_pa_t_kernel(tc, x_l, W_l_words, W_l_scales, b_l, W_
             )
 
         def layer2_block(block):
-            window, place = divmod(block, WINDOW)
+            group, place = divmod(block, GROUP)
             tokens = slice(place * P, (place + 1) * P)
             result = results.tile([P, OUT_COLUMNS], F32, name="result")
             for k, copy in enumerate((nc.scalar.copy, nc.vector.tensor_copy)):
@@ -247,8 +252,8 @@ def tile_bilinearpairedlayer_pa_t_kernel(tc, x_l, W_l_words, W_l_scales, b_l, W_
                 product = psum_2.tile([P, BANK], F32, name="product", tag="product")
                 nc.tensor.matmul_mx(
                     out=product[:],
-                    lhsT=hq_words[:, window % HQ_RING, tokens].bitcast(FP8X4),
-                    lhsT_scale=hq_scales[:, window % HQ_RING, tokens],
+                    lhsT=hq_words[:, group % HQ_RING, tokens].bitcast(FP8X4),
+                    lhsT_scale=hq_scales[:, group % HQ_RING, tokens],
                     rhs=wbq_words[:, columns].bitcast(FP8X4),
                     rhs_scale=wbq_scales[:, columns],
                     start=True,
@@ -277,22 +282,18 @@ def tile_bilinearpairedlayer_pa_t_kernel(tc, x_l, W_l_words, W_l_scales, b_l, W_
 
         next_block = 0
         last = len(STEPS) - 1
-        for step in range(len(STEPS) + LAYER2_LAG):
-            complete = None
-            if 1 <= step <= last + 1:
-                first, blocks, chunk0, chunks = STEPS[step - 1]
-                if chunk0 + chunks == H_CHUNKS:
-                    complete = (first, blocks)
-            if complete:
-                regroup_hidden(*complete)
+        for step in range(len(STEPS) + 8):
+            hidden = [(block, blocks) for block, blocks, ready in HALVES if ready == step]
+            for half in hidden:
+                regroup_hidden(*half)
             for start, pairs in RUNS:
                 if 1 <= step - start <= len(pairs):
                     quantise_pair(pairs[step - start - 1])
                 for i, pair in enumerate(pairs):
-                    if step == start - 2 - (len(pairs) - 1 - i) * 2 and pair in SPLIT_PAIRS:
+                    if step == start - 2 - (len(pairs) - 1 - i) and pair in SPLIT_PAIRS:
                         split_pair(pair)
-            if complete:
-                quantise_hidden(*complete)
+            for half in hidden:
+                quantise_hidden(*half)
             if step == 0:
                 layer1_bank(*STEPS[step])
             piece = step - FIRST_W_BIL_STEP
@@ -302,13 +303,12 @@ def tile_bilinearpairedlayer_pa_t_kernel(tc, x_l, W_l_words, W_l_scales, b_l, W_
                 if step == start:
                     for pair in pairs:
                         transpose_pair(pair)
-                        empty_pair(pair)
-
+                        empty_pair(pair, nc.vector.tensor_copy if pair % 2 else nc.scalar.copy)
             if 0 < step <= last:
                 layer1_bank(*STEPS[step])
             if 0 <= piece - 1 < W_BIL_PIECES:
                 quantise_w_bil(piece - 1)
             for turn in range(2):
-                if step >= FIRST_LAYER2_STEP and next_block < BLOCKS and (next_block + 4 <= step if step < 26 else (next_block if next_block >= BLOCKS - 4 else next_block // 2 * 2 + 1) + 2 <= step):
+                if step >= FIRST_LAYER2_STEP and next_block < BLOCKS and READY[next_block] + (2 if step < 26 else 1) <= step:
                     layer2_block(next_block)
                     next_block += 1

@@ -232,7 +232,7 @@ def tile_bilinearpairedlayer_pa_t_kernel(tc, x_l, W_l_words, W_l_scales, b_l, W_
             regroup(
                 wb_grouped[:, piece * W_BIL_PIECE : (piece + 1) * W_BIL_PIECE, :],
                 wb_raw[:, k, :, place : place + W_BIL_PIECE],
-                nc.vector.tensor_copy,
+                nc.scalar.copy if piece % 2 else nc.vector.tensor_copy,
             )
 
         def quantise_w_bil(piece):
@@ -290,7 +290,7 @@ def tile_bilinearpairedlayer_pa_t_kernel(tc, x_l, W_l_words, W_l_scales, b_l, W_
                 if 1 <= step - start <= len(pairs):
                     quantise_pair(pairs[step - start - 1])
                 for i, pair in enumerate(pairs):
-                    if step == start - 2 - (len(pairs) - 1 - i) and pair in SPLIT_PAIRS:
+                    if step == start - 3 - (len(pairs) - 1 - i) and pair in SPLIT_PAIRS:
                         split_pair(pair)
             for half in hidden:
                 quantise_hidden(*half)
@@ -309,6 +309,6 @@ def tile_bilinearpairedlayer_pa_t_kernel(tc, x_l, W_l_words, W_l_scales, b_l, W_
             if 0 <= piece - 1 < W_BIL_PIECES:
                 quantise_w_bil(piece - 1)
             for turn in range(2):
-                if step >= FIRST_LAYER2_STEP and next_block < BLOCKS and READY[next_block] + (2 if step < 26 else 1) <= step:
+                if step >= FIRST_LAYER2_STEP and next_block < BLOCKS and READY[next_block] + (2 if step < 28 else 1) <= step:
                     layer2_block(next_block)
                     next_block += 1

@@ -25,7 +25,7 @@ TOKENS = SEQUENCES * POSITIONS
 BLOCKS = TOKENS // P
 SEGMENTS_PER_SEQUENCE = POSITIONS // BLOCKS
 SLOTS = BLOCKS + 2
-PAIRS = SLOTS // 2
+PAIRS = BLOCKS // 2
 GROUP = 4
 GROUP_TOKENS = GROUP * P
 H_CHUNKS = HIDDEN // P
@@ -47,7 +47,7 @@ FIRST_LAYER2_STEP = 6
 FIRST_W_BIL_STEP = 1
 W_BIL_PIECES = 4
 W_BIL_PIECE = OUT_COLUMNS // W_BIL_PIECES
-RUNS = ((0, (2, 3,)), (2, (4, 5,)), (6, (6, 7,)), (10, (8, 9,)), (14, (10, 11,)), (18, (12, 13,)), (22, (14, 15,)), (26, (16,)))
+RUNS = ((0, (2, 3,)), (2, (4, 5,)), (6, (6, 7,)), (10, (8, 9,)), (14, (10, 11,)), (18, (12, 13,)), (22, (14, 15,)))
 SPLIT_PAIRS = range(8, PAIRS)
 X_RING = 6
 HQ_RING = 4
@@ -81,8 +81,6 @@ def tile_bilinearpairedlayer_pa_t_kernel(tc, x_l, W_l_words, W_l_scales, b_l, W_
         wbq_scales = keep.tile([P, OUT_COLUMNS], U8, align_bytes=64)
         zeros = keep.tile([P, BANK], BF16)
         identity = keep.tile([P, P], F32)
-        to_next_segment = keep.tile([P, P], F32)
-        to_previous_segment = keep.tile([P, P], F32)
         bias = keep.tile([P, H_CHUNKS], BF16)
         x_split = keep.tile([P, BLOCKS, 2, P], F32)
         x_grouped = keep.tile([P, X_RING, 2, P, PACK], BF16, align_bytes=64)
@@ -93,20 +91,12 @@ def tile_bilinearpairedlayer_pa_t_kernel(tc, x_l, W_l_words, W_l_scales, b_l, W_
         x_words = x_sb[:].bitcast(F32)
 
         nc.vector.memset(w_raw_scales[:].bitcast(I32), 0)
-        nc.vector.memset(to_next_segment[:], 0.0)
-        nc.vector.memset(to_previous_segment[:], 0.0)
+        for slot in (0, SLOTS - 1):
+            nc.vector.memset(xq_words[:].bitcast(I32)[:, slot * P : (slot + 1) * P], 0)
+            nc.vector.memset(xq_scales[:, slot * P : (slot + 1) * P], 0)
         nc.gpsimd.memset(zeros[:], 0.0)
         make_identity(nc, identity[:])
         nc.gpsimd.dma_start(out=bias[:], in_=b_l.rearrange("(p t) -> p t", t=H_CHUNKS))
-        by_sequence = "p (b s) -> p b s"
-        nc.vector.tensor_copy(
-            out=to_next_segment[:].rearrange(by_sequence, s=SEGMENTS_PER_SEQUENCE)[:, :, 1:],
-            in_=identity[:].rearrange(by_sequence, s=SEGMENTS_PER_SEQUENCE)[:, :, : SEGMENTS_PER_SEQUENCE - 1],
-        )
-        nc.vector.tensor_copy(
-            out=to_previous_segment[:].rearrange(by_sequence, s=SEGMENTS_PER_SEQUENCE)[:, :, : SEGMENTS_PER_SEQUENCE - 1],
-            in_=identity[:].rearrange(by_sequence, s=SEGMENTS_PER_SEQUENCE)[:, :, 1:],
-        )
 
         def load_blocks(blocks):
             nc.sync.dma_start(out=x_sb[:, blocks, :], in_=x_blocks[:, blocks, :])
@@ -134,40 +124,46 @@ def tile_bilinearpairedlayer_pa_t_kernel(tc, x_l, W_l_words, W_l_scales, b_l, W_
         load_blocks(slice(7, 11))
         for k in range(MAPS):
             nc.sync.dma_start(out=wb_raw[:, k], in_=W_bil[k].rearrange("(p t) g -> p t g", t=PACK))
-        for pair in range(6, PAIRS - 1):
+        for pair in range(6, PAIRS):
             load_pair(pair)
 
-        def slot_source(slot):
-            if slot == 0:
-                return BLOCKS - 1, to_next_segment
-            if slot == SLOTS - 1:
-                return 0, to_previous_segment
-            return slot - 1, identity
+        def pair_blocks(pair):
+            return (2 * pair - 1, 2 * pair) if pair else (0, BLOCKS - 1)
 
         def split_pair(pair):
-            blocks = slice(2 * pair - 1, 2 * pair + 1) if pair < PAIRS - 1 else slice(0, BLOCKS, BLOCKS - 1)
+            blocks = slice(2 * pair - 1, 2 * pair + 1)
             nc.vector.tensor_copy(
                 out=x_split[:, blocks], in_=x_words[:, blocks].rearrange("p b (w u) -> p b u w", u=2)
             )
 
         def transpose_pair(pair):
             bank = banks[pair] = psum_t.tile([P, 2, 2, P], F32, name="bank", tag="transposed")
-            for b in range(2):
-                block, permutation = slot_source(2 * pair + b)
+            for b, block in enumerate(pair_blocks(pair)):
                 for u in range(2):
                     words = x_split[:, block, u, :] if pair in SPLIT_PAIRS else x_words[:, block, u:X_WORDS:2]
-                    nc.tensor.transpose(out=bank[:, b, u, :], in_=words, identity=permutation[:])
+                    nc.tensor.transpose(out=bank[:, b, u, :], in_=words, identity=identity[:])
 
         def empty_pair(pair, copy=nc.scalar.copy):
             copy(out=x_grouped[:, pair % X_RING].bitcast(F32), in_=banks[pair][:].rearrange("p b u w -> p b w u"))
 
         def quantise_pair(pair):
-            columns = slice(2 * pair * P, (2 * pair + 2) * P)
-            nc.vector.quantize_mx(
-                out=xq_words[:, columns].bitcast(FP8X4),
-                scales=xq_scales[:, columns],
-                in_=x_grouped[:, pair % X_RING].rearrange("p b w t -> p (b w t)"),
-            )
+            first, second = pair_blocks(pair)
+            runs = [(0, 2, first)] if second == first + 1 else [(0, 1, first), (1, 2, second)]
+            for start, stop, block in runs:
+                columns = slice((block + 1) * P, (block + 1 + stop - start) * P)
+                nc.vector.quantize_mx(
+                    out=xq_words[:, columns].bitcast(FP8X4),
+                    scales=xq_scales[:, columns],
+                    in_=x_grouped[:, pair % X_RING, start:stop].rearrange("p b w t -> p (b w t)"),
+                )
+
+        def move_slot(source, target, taken, put):
+            by_sequence = "p (b s) -> p b s"
+            for tile in (xq_words[:].bitcast(I32), xq_scales[:]):
+                nc.vector.tensor_copy(
+                    out=tile[:, target * P : (target + 1) * P].rearrange(by_sequence, s=SEGMENTS_PER_SEQUENCE)[:, :, put],
+                    in_=tile[:, source * P : (source + 1) * P].rearrange(by_sequence, s=SEGMENTS_PER_SEQUENCE)[:, :, taken],
+                )
 
         def permute_weight(tap, half):
             by_unit, by_chunk = "p (m t) -> p t m", "p (t m) -> p t m"
@@ -275,6 +271,7 @@ def tile_bilinearpairedlayer_pa_t_kernel(tc, x_l, W_l_words, W_l_scales, b_l, W_
         quantise_pair(0)
         permute_weight(0, 0)
         quantise_pair(1)
+        move_slot(SLOTS - 2, 0, slice(0, SEGMENTS_PER_SEQUENCE - 1), slice(1, SEGMENTS_PER_SEQUENCE))
         permute_weight(1, 0)
         permute_weight(2, 0)
         for tap in range(TAPS):
@@ -292,8 +289,12 @@ def tile_bilinearpairedlayer_pa_t_kernel(tc, x_l, W_l_words, W_l_scales, b_l, W_
                 for i, pair in enumerate(pairs):
                     if step == start - 3 - (len(pairs) - 1 - i) and pair in SPLIT_PAIRS:
                         split_pair(pair)
-            for half in hidden:
-                quantise_hidden(*half)
+            if step >= 28 - 2:
+                for half in hidden:
+                    quantise_hidden(*half)
+                hidden = []
+            if step == 20:
+                move_slot(1, SLOTS - 1, slice(1, SEGMENTS_PER_SEQUENCE), slice(0, SEGMENTS_PER_SEQUENCE - 1))
             if step == 0:
                 layer1_bank(*STEPS[step])
             piece = step - FIRST_W_BIL_STEP
@@ -309,6 +310,8 @@ def tile_bilinearpairedlayer_pa_t_kernel(tc, x_l, W_l_words, W_l_scales, b_l, W_
             if 0 <= piece - 1 < W_BIL_PIECES:
                 quantise_w_bil(piece - 1)
             for turn in range(2):
-                if step >= FIRST_LAYER2_STEP and next_block < BLOCKS and READY[next_block] + (2 if step < 28 else 1) <= step:
+                if step >= FIRST_LAYER2_STEP and next_block < BLOCKS and READY[next_block] + (3 if step < 28 else 1) <= step:
                     layer2_block(next_block)
                     next_block += 1
+            for half in hidden:
+                quantise_hidden(*half)

@@ -228,7 +228,7 @@ def tile_bilinearpairedlayer_pa_t_kernel(tc, x_l, W_l_words, W_l_scales, b_l, W_
             regroup(
                 wb_grouped[:, piece * W_BIL_PIECE : (piece + 1) * W_BIL_PIECE, :],
                 wb_raw[:, k, :, place : place + W_BIL_PIECE],
-                nc.scalar.copy if piece % 2 else nc.vector.tensor_copy,
+                nc.vector.tensor_copy,
             )
 
         def quantise_w_bil(piece):
@@ -289,10 +289,8 @@ def tile_bilinearpairedlayer_pa_t_kernel(tc, x_l, W_l_words, W_l_scales, b_l, W_
                 for i, pair in enumerate(pairs):
                     if step == start - 3 - (len(pairs) - 1 - i) and pair in SPLIT_PAIRS:
                         split_pair(pair)
-            if step >= 28 - 2:
-                for half in hidden:
-                    quantise_hidden(*half)
-                hidden = []
+            for half in hidden:
+                quantise_hidden(*half)
             if step == 20:
                 move_slot(1, SLOTS - 1, slice(1, SEGMENTS_PER_SEQUENCE), slice(0, SEGMENTS_PER_SEQUENCE - 1))
             if step == 0:
@@ -304,14 +302,12 @@ def tile_bilinearpairedlayer_pa_t_kernel(tc, x_l, W_l_words, W_l_scales, b_l, W_
                 if step == start:
                     for pair in pairs:
                         transpose_pair(pair)
-                        empty_pair(pair, nc.vector.tensor_copy if pair % 2 else nc.scalar.copy)
+                        empty_pair(pair, nc.vector.tensor_copy if pair >= 8 and pair % 2 else nc.scalar.copy)
             if 0 < step <= last:
                 layer1_bank(*STEPS[step])
             if 0 <= piece - 1 < W_BIL_PIECES:
                 quantise_w_bil(piece - 1)
             for turn in range(2):
-                if step >= FIRST_LAYER2_STEP and next_block < BLOCKS and READY[next_block] + (3 if step < 28 else 1) <= step:
+                if step >= FIRST_LAYER2_STEP and next_block < BLOCKS and READY[next_block] + (2 if step < 26 else 1) <= step:
                     layer2_block(next_block)
                     next_block += 1
-            for half in hidden:
-                quantise_hidden(*half)

@@ -13,6 +13,7 @@ RELU = mybir.ActivationFunctionType.Relu
 
 P = 128
 PACK = 4
+LINE_BYTES = 64
 BANK = 512
 
 SEQUENCES = 8
@@ -69,16 +70,21 @@ def tile_bilinearpairedlayer_pa_t_kernel(tc, x_l, W_l_words, W_l_scales, b_l, W_
         psum_2 = ctx.enter_context(tc.psum_pool(name="psum_2", bufs=4))
 
         x_sb = keep.tile([P, BLOCKS, FEATURES], BF16)
-        xq_words = keep.tile([P, SLOTS * P], U32, align_bytes=64)
-        xq_scales = keep.tile([P, SLOTS * P], U8, align_bytes=64)
-        w_words = keep.tile([P, TAPS, HIDDEN], U32, align_bytes=64)
-        w_scales = keep.tile([P, TAPS, HIDDEN], U8, align_bytes=64)
+        def operand(name, columns, dtype, line):
+            skip = line * LINE_BYTES // (4 if dtype == U32 else 1)
+            return keep.tile([P, skip + columns], dtype, name=name, align_bytes=4 * LINE_BYTES)[:, skip:]
+
+        xq_words = operand("xq_words", SLOTS * P, U32, 0)
+        xq_scales = operand("xq_scales", SLOTS * P, U8, 1)
+        by_tap = "p (g n) -> p g n"
+        w_words = operand("w_words", TAPS * HIDDEN, U32, 2).rearrange(by_tap, g=TAPS)
+        w_scales = operand("w_scales", TAPS * HIDDEN, U8, 3).rearrange(by_tap, g=TAPS)
         w_raw_words = keep.tile([P, TAPS, HIDDEN], U32, align_bytes=64)
         w_raw_scales = keep.tile([P, TAPS, HIDDEN], U8, align_bytes=64)
         wb_raw = keep.tile([P, MAPS, PACK, HIDDEN], BF16)
         wb_grouped = keep.tile([P, OUT_COLUMNS, PACK], BF16, align_bytes=64)
-        wbq_words = keep.tile([P, OUT_COLUMNS], U32, align_bytes=64)
-        wbq_scales = keep.tile([P, OUT_COLUMNS], U8, align_bytes=64)
+        wbq_words = operand("wbq_words", OUT_COLUMNS, U32, 0)
+        wbq_scales = operand("wbq_scales", OUT_COLUMNS, U8, 1)
         zeros = keep.tile([P, BANK], BF16)
         identity = keep.tile([P, P], F32)
         bias = keep.tile([P, H_CHUNKS], BF16)
@@ -86,8 +92,9 @@ def tile_bilinearpairedlayer_pa_t_kernel(tc, x_l, W_l_words, W_l_scales, b_l, W_
         x_grouped = keep.tile([P, X_RING, 2, P, PACK], BF16, align_bytes=64)
         h_planes = keep.tile([P, 2, H_CHUNKS, GROUP_TOKENS], BF16)
         h_grouped = keep.tile([P, 2, GROUP_TOKENS, PACK], BF16, align_bytes=64)
-        hq_words = keep.tile([P, HQ_RING, GROUP_TOKENS], U32, align_bytes=64)
-        hq_scales = keep.tile([P, HQ_RING, GROUP_TOKENS], U8, align_bytes=64)
+        by_group = "p (q w) -> p q w"
+        hq_words = operand("hq_words", HQ_RING * GROUP_TOKENS, U32, 2).rearrange(by_group, q=HQ_RING)
+        hq_scales = operand("hq_scales", HQ_RING * GROUP_TOKENS, U8, 3).rearrange(by_group, q=HQ_RING)
         x_words = x_sb[:].bitcast(F32)
 
         nc.vector.memset(w_raw_scales[:].bitcast(I32), 0)

from contextlib import ExitStack

import concourse.mybir as mybir
from concourse.masks import make_identity

F32 = mybir.dt.float32
BF16 = mybir.dt.bfloat16
I32 = mybir.dt.int32
U32 = mybir.dt.uint32
U8 = mybir.dt.uint8
FP8X4 = mybir.dt.float8_e4m3fn_x4
RELU = mybir.ActivationFunctionType.Relu

P = 128
PACK = 4
LINE_BYTES = 64
BANK = 512

SEQUENCES = 8
POSITIONS = 512
FEATURES = 512
HIDDEN = 512
MAPS = 2
TAPS = 3
TOKENS = SEQUENCES * POSITIONS
BLOCKS = TOKENS // P
SEGMENTS_PER_SEQUENCE = POSITIONS // BLOCKS
SLOTS = BLOCKS + 2
PAIRS = BLOCKS // 2
GROUP = 4
GROUP_TOKENS = GROUP * P
H_CHUNKS = HIDDEN // P
X_WORDS = FEATURES // 2
OUT_COLUMNS = MAPS * HIDDEN

TAP_SLOT = (1, 0, 2)

WINDOWS = ((0, 2), (2, 2), (4, 2), (6, 2), (8, 2), (10, 2), (12, 2), (14, 2), (16, 2), (18, 2), (20, 2), (22, 2), (24, 2), (26, 2), (28, 1), (29, 1), (30, 1), (31, 1))
STEPS = [(first, blocks, chunk, 4 // blocks) for first, blocks in WINDOWS for chunk in range(0, H_CHUNKS, 4 // blocks)]
FINISHED = [(i, first, blocks) for i, (first, blocks, chunk, chunks) in enumerate(STEPS) if chunk + chunks == H_CHUNKS]
HALVES = [
    (first + part, min(blocks, 2), i + 1 + part // 2)
    for i, first, blocks in FINISHED
    for part in range(0, blocks, 2)
]
READY = {first + k: ready for first, blocks, ready in HALVES for k in range(blocks)}
FIRST_LAYER2_STEP = 6
FIRST_W_BIL_STEP = 1
W_BIL_PIECES = 4
W_BIL_PIECE = OUT_COLUMNS // W_BIL_PIECES
RUNS = ((0, (2, 3,)), (2, (4, 5,)), (6, (6, 7,)), (10, (8, 9,)), (14, (10, 11,)), (18, (12, 13,)), (22, (14, 15,)))
SPLIT_PAIRS = range(8, PAIRS)
X_RING = 6
HQ_RING = 4

FLOPS = 2 * TOKENS * (TAPS * FEATURES * HIDDEN + HIDDEN * OUT_COLUMNS)


def tile_bilinearpairedlayer_pa_t_kernel(tc, x_l, W_l_words, W_l_scales, b_l, W_bil, out):
    nc = tc.nc
    x_blocks = x_l.rearrange("b (s r) f -> (b s) r f", r=BLOCKS)
    out_blocks = out.rearrange("b (s r) k g -> (b s) r (k g)", r=BLOCKS)

    with ExitStack() as ctx:
        ctx.enter_context(tc.manual_schedule())
        keep = ctx.enter_context(tc.tile_pool(name="keep", bufs=1))
        results = ctx.enter_context(tc.tile_pool(name="results", bufs=8))
        psum_t = ctx.enter_context(tc.psum_pool(name="psum_t", bufs=2))
        psum_1 = ctx.enter_context(tc.psum_pool(name="psum_1", bufs=2))
        psum_2 = ctx.enter_context(tc.psum_pool(name="psum_2", bufs=4))

        x_sb = keep.tile([P, BLOCKS, FEATURES], BF16)
        def operand(name, columns, dtype, line):
            skip = line * LINE_BYTES // (4 if dtype == U32 else 1)
            return keep.tile([P, skip + columns], dtype, name=name, align_bytes=4 * LINE_BYTES)[:, skip:]

        xq_words = operand("xq_words", SLOTS * P, U32, 0)
        xq_scales = operand("xq_scales", SLOTS * P, U8, 1)
        by_tap = "p (g n) -> p g n"
        w_words = operand("w_words", TAPS * HIDDEN, U32, 2).rearrange(by_tap, g=TAPS)
        w_scales = operand("w_scales", TAPS * HIDDEN, U8, 3).rearrange(by_tap, g=TAPS)
        w_raw_words = keep.tile([P, TAPS, HIDDEN], U32, align_bytes=64)
        w_raw_scales = keep.tile([P, TAPS, HIDDEN], U8, align_bytes=64)
        wb_raw = keep.tile([P, MAPS, PACK, HIDDEN], BF16)
        wb_grouped = keep.tile([P, OUT_COLUMNS, PACK], BF16, align_bytes=64)
        wbq_words = operand("wbq_words", OUT_COLUMNS, U32, 0)
        wbq_scales = operand("wbq_scales", OUT_COLUMNS, U8, 1)
        zeros = keep.tile([P, BANK], BF16)
        identity = keep.tile([P, P], F32)
        bias = keep.tile([P, H_CHUNKS], BF16)
        x_split = keep.tile([P, BLOCKS, 2, P], F32)
        x_grouped = keep.tile([P, X_RING, 2, P, PACK], BF16, align_bytes=64)
        h_planes = keep.tile([P, 2, H_CHUNKS, GROUP_TOKENS], BF16)
        h_grouped = keep.tile([P, 2, GROUP_TOKENS, PACK], BF16, align_bytes=64)
        by_group = "p (q w) -> p q w"
        hq_words = operand("hq_words", HQ_RING * GROUP_TOKENS, U32, 2).rearrange(by_group, q=HQ_RING)
        hq_scales = operand("hq_scales", HQ_RING * GROUP_TOKENS, U8, 3).rearrange(by_group, q=HQ_RING)
        x_words = x_sb[:].bitcast(F32)

        nc.vector.memset(w_raw_scales[:].bitcast(I32), 0)
        for slot in (0, SLOTS - 1):
            nc.vector.memset(xq_words[:].bitcast(I32)[:, slot * P : (slot + 1) * P], 0)
            nc.vector.memset(xq_scales[:, slot * P : (slot + 1) * P], 0)
        nc.gpsimd.memset(zeros[:], 0.0)
        make_identity(nc, identity[:])
        nc.gpsimd.dma_start(out=bias[:], in_=b_l.rearrange("(p t) -> p t", t=H_CHUNKS))

        def load_blocks(blocks):
            nc.sync.dma_start(out=x_sb[:, blocks, :], in_=x_blocks[:, blocks, :])

        def load_pair(pair):
            load_blocks(slice(2 * pair - 1, 2 * pair + 1))

        def load_weight(taps):
            nc.sync.dma_start(
                out=w_raw_words[:, taps, :].bitcast(I32),
                in_=W_l_words[taps].rearrange("g p n t -> p g (n t)").bitcast(I32),
            )

        load_blocks(slice(0, BLOCKS, BLOCKS - 1))
        load_pair(1)
        for quadrant in range(4):
            nc.sync.dma_start(
                out=w_raw_scales[32 * quadrant : 32 * quadrant + 4, :, :].bitcast(I32),
                in_=W_l_scales[:, 4 * quadrant : 4 * quadrant + 4, :].rearrange("g r n -> r g n").bitcast(I32),
            )
        load_weight(slice(0, 1))
        load_weight(slice(1, 2))
        load_weight(slice(2, 3))
        load_blocks(slice(3, 7))
        load_blocks(slice(7, 11))
        for k in range(MAPS):
            nc.sync.dma_start(out=wb_raw[:, k], in_=W_bil[k].rearrange("(p t) g -> p t g", t=PACK))
        for pair in range(6, PAIRS):
            load_pair(pair)

        def pair_blocks(pair):
            return (2 * pair - 1, 2 * pair) if pair else (0, BLOCKS - 1)

        def split_pair(pair):
            blocks = slice(2 * pair - 1, 2 * pair + 1)
            nc.vector.tensor_copy(
                out=x_split[:, blocks], in_=x_words[:, blocks].rearrange("p b (w u) -> p b u w", u=2)
            )

        def transpose_pair(pair):
            bank = banks[pair] = psum_t.tile([P, 2, 2, P], F32, name="bank", tag="transposed")
            for b, block in enumerate(pair_blocks(pair)):
                for u in range(2):
                    words = x_split[:, block, u, :] if pair in SPLIT_PAIRS else x_words[:, block, u:X_WORDS:2]
                    nc.tensor.transpose(out=bank[:, b, u, :], in_=words, identity=identity[:])

        def empty_pair(pair, copy=nc.scalar.copy):
            copy(out=x_grouped[:, pair % X_RING].bitcast(F32), in_=banks[pair][:].rearrange("p b u w -> p b w u"))

        def quantise_pair(pair):
            first, second = pair_blocks(pair)
            runs = [(0, 2, first)] if second == first + 1 else [(0, 1, first), (1, 2, second)]
            for start, stop, block in runs:
                columns = slice((block + 1) * P, (block + 1 + stop - start) * P)
                nc.vector.quantize_mx(
                    out=xq_words[:, columns].bitcast(FP8X4),
                    scales=xq_scales[:, columns],
                    in_=x_grouped[:, pair % X_RING, start:stop].rearrange("p b w t -> p (b w t)"),
                )

        def move_slot(source, target, taken, put):
            by_sequence = "p (b s) -> p b s"
            for tile in (xq_words[:].bitcast(I32), xq_scales[:]):
                nc.vector.tensor_copy(
                    out=tile[:, target * P : (target + 1) * P].rearrange(by_sequence, s=SEGMENTS_PER_SEQUENCE)[:, :, put],
                    in_=tile[:, source * P : (source + 1) * P].rearrange(by_sequence, s=SEGMENTS_PER_SEQUENCE)[:, :, taken],
                )

        def permute_weight(tap, half):
            by_unit, by_chunk = "p (m t) -> p t m", "p (t m) -> p t m"
            chunks = slice(2 * half, 2 * half + 2)
            nc.vector.tensor_copy(
                out=w_words[:, tap, :].bitcast(I32).rearrange(by_chunk, t=H_CHUNKS)[:, chunks],
                in_=w_raw_words[:, tap, :].bitcast(I32).rearrange(by_unit, t=H_CHUNKS)[:, chunks],
            )
            nc.vector.tensor_copy(
                out=w_scales[:, tap, :].rearrange(by_chunk, t=H_CHUNKS)[:, chunks],
                in_=w_raw_scales[:, tap, :].rearrange(by_unit, t=H_CHUNKS)[:, chunks],
            )

        def keep_warm(count):
            for turn in range(count):
                scratch = psum_2.tile([P, BANK], F32, name="scratch", tag="product")
                nc.tensor.matmul(out=scratch[:], lhsT=zeros[:, 0:P], rhs=zeros[:], start=True, stop=True)

        def layer1_bank(first, blocks, chunk0, chunks):
            tokens = blocks * P
            groups = psum_1.tile([P, chunks, tokens], F32, name="groups")
            for i in range(chunks):
                units = slice((chunk0 + i) * P, (chunk0 + i + 1) * P)
                for g in range(TAPS):
                    column = (first + TAP_SLOT[g]) * P
                    nc.tensor.matmul_mx(
                        out=groups[:, i, :],
                        lhsT=w_words[:, g, units].bitcast(FP8X4),
                        lhsT_scale=w_scales[:, g, units],
                        rhs=xq_words[:, column : column + tokens].bitcast(FP8X4),
                        rhs_scale=xq_scales[:, column : column + tokens],
                        start=(g == 0),
                        stop=(g == TAPS - 1),
                    )
            for i in range(chunks):
                chunk = chunk0 + i
                nc.scalar.activation(
                    out=h_planes[:, first // GROUP % 2, chunk, first % GROUP * P : first % GROUP * P + tokens],
                    in_=groups[:, i, :],
                    func=RELU,
                    bias=bias[:, chunk : chunk + 1],
                    scale=1.0,
                )

        def regroup(grouped, planes, copy=nc.vector.tensor_copy):
            copy(out=grouped.rearrange("p (c i) t -> p c t i", i=4), in_=planes.rearrange("p t (c i) -> p c t i", i=4))

        def regroup_hidden(first, blocks):
            columns = slice(first % GROUP * P, (first % GROUP + blocks) * P)
            regroup(h_grouped[:, first // GROUP % 2, columns], h_planes[:, first // GROUP % 2, :, columns])

        def quantise_hidden(first, blocks):
            columns = slice(first % GROUP * P, (first % GROUP + blocks) * P)
            nc.vector.quantize_mx(
                out=hq_words[:, first // GROUP % HQ_RING, columns].bitcast(FP8X4),
                scales=hq_scales[:, first // GROUP % HQ_RING, columns],
                in_=h_grouped[:, first // GROUP % 2, columns].rearrange("p w t -> p (w t)"),
            )

        def regroup_w_bil(piece):
            k, place = divmod(piece * W_BIL_PIECE, HIDDEN)
            regroup(
                wb_grouped[:, piece * W_BIL_PIECE : (piece + 1) * W_BIL_PIECE, :],
                wb_raw[:, k, :, place : place + W_BIL_PIECE],
                nc.vector.tensor_copy,
            )

        def quantise_w_bil(piece):
            columns = slice(piece * W_BIL_PIECE, (piece + 1) * W_BIL_PIECE)
            nc.vector.quantize_mx(
                out=wbq_words[:, columns].bitcast(FP8X4),
                scales=wbq_scales[:, columns],
                in_=wb_grouped[:, columns, :].rearrange("p n t -> p (n t)"),
            )

        def layer2_block(block):
            group, place = divmod(block, GROUP)
            tokens = slice(place * P, (place + 1) * P)
            result = results.tile([P, OUT_COLUMNS], F32, name="result")
            for k, copy in enumerate((nc.scalar.copy, nc.vector.tensor_copy)):
                columns = slice(k * HIDDEN, (k + 1) * HIDDEN)
                product = psum_2.tile([P, BANK], F32, name="product", tag="product")
                nc.tensor.matmul_mx(
                    out=product[:],
                    lhsT=hq_words[:, group % HQ_RING, tokens].bitcast(FP8X4),
                    lhsT_scale=hq_scales[:, group % HQ_RING, tokens],
                    rhs=wbq_words[:, columns].bitcast(FP8X4),
                    rhs_scale=wbq_scales[:, columns],
                    start=True,
                    stop=True,
                )
                copy(out=result[:, columns], in_=product[:])
            pieces = 1 if block < BLOCKS - 2 else MAPS
            for piece in range(pieces):
                columns = slice(piece * OUT_COLUMNS // pieces, (piece + 1) * OUT_COLUMNS // pieces)
                nc.sync.dma_start(out=out_blocks[:, block, columns], in_=result[:, columns])

        banks = {}
        keep_warm(3)
        transpose_pair(0)
        empty_pair(0)
        transpose_pair(1)
        empty_pair(1)
        keep_warm(4)
        quantise_pair(0)
        permute_weight(0, 0)
        quantise_pair(1)
        move_slot(SLOTS - 2, 0, slice(0, SEGMENTS_PER_SEQUENCE - 1), slice(1, SEGMENTS_PER_SEQUENCE))
        permute_weight(1, 0)
        permute_weight(2, 0)
        for tap in range(TAPS):
            permute_weight(tap, 1)

        next_block = 0
        last = len(STEPS) - 1
        for step in range(len(STEPS) + 8):
            hidden = [(block, blocks) for block, blocks, ready in HALVES if ready == step]
            for half in hidden:
                regroup_hidden(*half)
            for start, pairs in RUNS:
                if 1 <= step - start <= len(pairs):
                    quantise_pair(pairs[step - start - 1])
                for i, pair in enumerate(pairs):
                    if step == start - 3 - (len(pairs) - 1 - i) and pair in SPLIT_PAIRS:
                        split_pair(pair)
            for half in hidden:
                quantise_hidden(*half)
            if step == 20:
                move_slot(1, SLOTS - 1, slice(1, SEGMENTS_PER_SEQUENCE), slice(0, SEGMENTS_PER_SEQUENCE - 1))
            if step == 0:
                layer1_bank(*STEPS[step])
            piece = step - FIRST_W_BIL_STEP
            if 0 <= piece < W_BIL_PIECES:
                regroup_w_bil(piece)
            for start, pairs in RUNS:
                if step == start:
                    for pair in pairs:
                        transpose_pair(pair)
                        empty_pair(pair, nc.vector.tensor_copy if pair >= 8 and pair % 2 else nc.scalar.copy)
            if 0 < step <= last:
                layer1_bank(*STEPS[step])
            if 0 <= piece - 1 < W_BIL_PIECES:
                quantise_w_bil(piece - 1)
            for turn in range(2):
                if step >= FIRST_LAYER2_STEP and next_block < BLOCKS and READY[next_block] + (2 if step < 26 else 1) <= step:
                    layer2_block(next_block)
                    next_block += 1
